import numpy as np
import ml_dtypes


def mxq(x, axis, fmt="e4m3"):
    dtype, down = {"e4m3": (ml_dtypes.float8_e4m3fn, 7), "e5m2": (ml_dtypes.float8_e5m2, 14)}[fmt]
    v = np.moveaxis(np.asarray(x, np.float32).astype(ml_dtypes.bfloat16).astype(np.float64), axis, -1)
    blocks = v.reshape(v.shape[:-1] + (-1, 32))
    amax = np.abs(blocks).max(-1, keepdims=True)
    byte = np.maximum(np.where(amax > 0, np.frexp(amax)[1] - 1 + 127, 0) - down, 1)
    scale = np.exp2(byte - 127.0)
    codes = (blocks / scale).astype(np.float32).astype(dtype).astype(np.float64)
    return np.moveaxis((codes * scale).reshape(v.shape), -1, axis)


WIDE = False


def mx_kscale(k):
    if not WIDE:
        return np.ones(k)
    levels = np.array([10, -10, 5, -5, 0])
    if k % 512:
        return np.exp2(np.random.permutation(np.resize(levels, k // 32))).repeat(32)
    a = np.empty((k // 512, 16))
    for p in range(k // 512):
        a[p, :8] = np.random.permutation(np.resize(levels, 8))
        for g in range(8):
            far = levels[np.abs(levels - a[p, g]) >= 10]
            a[p, g + 8] = far[np.random.randint(len(far))]
    return np.exp2(a.ravel()).repeat(32)


BF16 = ml_dtypes.bfloat16


def bf(x):
    return np.asarray(x, np.float32).astype(BF16)


def f64(x):
    return np.asarray(x).astype(np.float64)


B, I, H, P = 512, 16128, 256, 2048
C = I + H


def sigmoid(v):
    return 1.0 / (1.0 + np.exp(-v))


def setup_inputs():
    s = mx_kscale(C)
    return {"x": bf(np.random.standard_normal((B, I)) * s[:I]),
            "rh": bf(np.random.standard_normal((B, H)) * 0.95 * s[I:]),
            "update": bf(np.random.standard_normal((B, H)) * 0.7),
            "hidden": bf(1.5 + np.random.standard_normal((B, H))),
            "Wn": bf(np.random.standard_normal((H, C)) / np.sqrt(C) / s[None, :]),
            "bn": bf(-0.1 + 0.2 * np.random.standard_normal(H)),
            "connection_strength": bf(1.0 + 0.3 * np.random.standard_normal(H)),
            "connection_decay": bf(0.4 + 0.2 * np.random.random(1)),
            "connection_history": bf(2.0 * np.random.standard_normal(H))}


def reference(x, rh, update, hidden, Wn, bn, connection_strength, connection_decay, connection_history):
    h = f64(hidden)
    u = f64(update)
    activity = np.mean(np.abs(h), axis=0)
    ch = f64(connection_history) * f64(connection_decay) + activity
    cs = f64(connection_strength) * sigmoid(ch)
    combined_reset = np.concatenate([f64(x), f64(rh)], axis=1)
    new = (mxq(combined_reset, 1, "e4m3") @ mxq(f64(Wn), 1, "e4m3").T) + f64(bn)
    return (1.0 - u) * h + u * new * cs[None, :]

@@ -1,0 +1,301 @@
+from contextlib import ExitStack
+
+import concourse.mybir as mybir
+from concourse.masks import make_identity
+
+FLOPS = 2 * 512 * 256 * 16384
+
+F32 = mybir.dt.float32
+BF16 = mybir.dt.bfloat16
+U32 = mybir.dt.uint32
+U8 = mybir.dt.uint8
+FP8X4 = mybir.dt.float8_e4m3fn_x4
+ALU = mybir.AluOpType
+ACT = mybir.ActivationFunctionType
+
+P = 128
+K_PASS = 512
+K_BLOCK = 256
+BANK = 512
+K_BANK = 4 * K_BLOCK
+CHUNK = 4096
+UNIT_BANKS = CHUNK // K_BANK
+CHUNK_PASSES = CHUNK // K_PASS
+STEP_K = 2048
+STEP_PASSES = STEP_K // K_PASS
+X_BANKS = STEP_K // K_BANK
+W_BANKS = X_BANKS // 2
+STEPS_PER_UNIT = CHUNK // STEP_K
+LAG = 2
+RAW_BUFS = 12
+
+
+def tile_persistentgrucell_pb_k_kernel(
+    tc,
+    x,
+    rh,
+    update,
+    hidden,
+    Wn,
+    bn,
+    connection_strength,
+    connection_decay,
+    connection_history,
+    out,
+):
+    nc = tc.nc
+    B, I = x.shape
+    H = rh.shape[1]
+    K = I + H
+    ROW_TILES = B // P
+    W_TILES = H // P
+    n_chunks = K // CHUNK
+    assert n_chunks > 3
+    assert ROW_TILES * STEPS_PER_UNIT * W_BANKS == W_TILES * UNIT_BANKS
+
+    x_rows = x.rearrange("(p t) k -> t p k", t=ROW_TILES)
+    rh_rows = rh.rearrange("(p t) c -> t p c", t=ROW_TILES)
+    out_rows = out.rearrange("(p t) h -> t p h", t=ROW_TILES)
+
+    stream = [("w", 0, j) for j in range(W_TILES)]
+    for c in range(n_chunks):
+        for j in range(W_TILES):
+            if c + 1 < n_chunks:
+                stream.append(("w", c + 1, j))
+            stream.extend([("x", c, t) for t in range(2 * j, 2 * j + 2)])
+    position = dict([(unit, n) for n, unit in enumerate(stream)])
+
+    steps = []
+    for c in range(n_chunks):
+        for t in range(ROW_TILES):
+            steps.extend([(c, t, h) for h in range(STEPS_PER_UNIT)])
+    n_steps = len(steps)
+
+    with ExitStack() as ctx:
+        ctx.enter_context(tc.manual_schedule())
+        const = ctx.enter_context(tc.tile_pool(name="const", bufs=1))
+        raw_pool = ctx.enter_context(tc.tile_pool(name="raw", bufs=RAW_BUFS))
+        stage = ctx.enter_context(tc.tile_pool(name="stage", bufs=LAG + 2))
+        w_pool = ctx.enter_context(tc.tile_pool(name="wq", bufs=3))
+        out_pool = ctx.enter_context(tc.tile_pool(name="outs", bufs=2))
+        acc_pool = ctx.enter_context(tc.psum_pool(name="acc", bufs=1))
+        bank_pool = ctx.enter_context(tc.psum_pool(name="banks", bufs=4))
+
+        def load(unit):
+            kind, c, r = unit
+            raw = raw_pool.tile([P, CHUNK], BF16, tag="raw")
+            k0 = c * CHUNK
+            if kind == "w":
+                nc.sync.dma_start(out=raw[:], in_=Wn[r * P : (r + 1) * P, k0 : k0 + CHUNK])
+            else:
+                width = min(CHUNK, I - k0)
+                nc.sync.dma_start(out=raw[:, 0:width], in_=x_rows[r][:, k0 : k0 + width])
+                if width < CHUNK:
+                    nc.sync.dma_start(out=raw[:, width:CHUNK], in_=rh_rows[r])
+            return raw
+
+        ident = const.tile([P, P], F32)
+        make_identity(nc, ident[:])
+        ones = const.tile([P, P], BF16)
+        nc.vector.memset(ones[:], 1.0)
+        vectors = const.tile([P, 2 * BANK], BF16)
+        nc.vector.memset(vectors[:], 0.0)
+        zero = const.tile([P, 1], F32)
+        nc.vector.memset(zero[:], 0.0)
+
+        raws = {}
+        for i in range(2):
+            raws[stream[i]] = load(stream[i])
+        hid = const.tile([P, ROW_TILES * H], BF16)
+        nc.scalar.dma_start(out=hid[:], in_=hidden.rearrange("(p t) h -> p (t h)", t=ROW_TILES))
+        nc.scalar.dma_start(out=vectors[0:1, 0:H], in_=bn.unsqueeze(0))
+        nc.scalar.dma_start(out=vectors[0:1, H : 2 * H], in_=connection_strength.unsqueeze(0))
+        nc.scalar.dma_start(out=vectors[0:1, BANK : BANK + H], in_=connection_history.unsqueeze(0))
+        nc.scalar.dma_start(
+            out=vectors[0:1, BANK + H : BANK + H + 1], in_=connection_decay.unsqueeze(0)
+        )
+        upd = const.tile([P, ROW_TILES * H], BF16)
+        nc.scalar.dma_start(out=upd[:], in_=update.rearrange("(p t) h -> p (t h)", t=ROW_TILES))
+        for i in range(2, RAW_BUFS):
+            raws[stream[i]] = load(stream[i])
+
+        warm = const.tile([P, 1], F32)
+        nc.scalar.activation(out=warm[:], in_=zero[:], func=ACT.Sigmoid)
+
+        habs = const.tile([P, ROW_TILES * H], BF16)
+        nc.vector.scalar_tensor_tensor(
+            out=habs[:], in0=hid[:], scalar=-1.0, in1=hid[:], op0=ALU.mult, op1=ALU.max
+        )
+        spread_a = acc_pool.tile([P, BANK], F32, tag="acc0")
+        nc.tensor.matmul(spread_a[:], lhsT=ones[:], rhs=vectors[:, 0:BANK], start=True, stop=True)
+        spread_b = acc_pool.tile([P, BANK], F32, tag="acc1")
+        nc.tensor.matmul(
+            spread_b[:], lhsT=ones[:], rhs=vectors[:, BANK : 2 * BANK], start=True, stop=True
+        )
+        abs_sum = acc_pool.tile([P, H], F32, tag="acc2")
+        for t in range(ROW_TILES):
+            nc.tensor.matmul(
+                abs_sum[:],
+                lhsT=ones[:],
+                rhs=habs[:, t * H : (t + 1) * H],
+                start=(t == 0),
+                stop=(t == ROW_TILES - 1),
+            )
+        keep = const.tile([P, ROW_TILES * H], F32)
+        nc.vector.tensor_tensor(out=keep[:], in0=upd[:], in1=hid[:], op=ALU.mult)
+        nc.vector.tensor_tensor(out=keep[:], in0=hid[:], in1=keep[:], op=ALU.subtract)
+        decay = const.tile([P, 1], F32)
+        nc.vector.tensor_copy(out=decay[:], in_=spread_b[:, H : H + 1])
+        ch = const.tile([P, H], F32)
+        nc.vector.tensor_scalar(
+            out=ch[:], in0=spread_b[:, 0:H], scalar1=decay[:, 0:1], scalar2=None, op0=ALU.mult
+        )
+        nc.vector.scalar_tensor_tensor(
+            out=ch[:], in0=abs_sum[:], scalar=1.0 / B, in1=ch[:], op0=ALU.mult, op1=ALU.add
+        )
+        sig = const.tile([P, H], F32)
+        nc.scalar.activation(out=sig[:], in_=ch[:], func=ACT.Sigmoid)
+        cs = const.tile([P, H], F32)
+        nc.vector.tensor_tensor(out=cs[:], in0=sig[:], in1=spread_a[:, H : 2 * H], op=ALU.mult)
+        cs_bn = const.tile([P, H], F32)
+        nc.vector.tensor_tensor(out=cs_bn[:], in0=cs[:], in1=spread_a[:, 0:H], op=ALU.mult)
+
+        gain = const.tile([P, ROW_TILES * H], F32)
+        bias = const.tile([P, ROW_TILES * H], F32)
+
+        def prepare_blend(step, t):
+            cols = slice(t * H, (t + 1) * H)
+            if step == 0:
+                nc.vector.tensor_tensor(out=gain[:, cols], in0=upd[:, cols], in1=cs[:], op=ALU.mult)
+            elif step == 1:
+                nc.vector.tensor_tensor(out=bias[:, cols], in0=upd[:, cols], in1=cs_bn[:], op=ALU.mult)
+            elif step == 2:
+                nc.vector.tensor_tensor(
+                    out=keep[:, cols], in0=keep[:, cols], in1=bias[:, cols], op=ALU.add
+                )
+
+        acc = [
+            acc_pool.tile([P, H], F32, name="acc%d" % t, tag="acc%d" % t) for t in range(ROW_TILES)
+        ]
+
+        def transpose_bank(blocks, grouped, on_vector):
+            bank = bank_pool.tile([P, BANK], F32, tag="bank")
+            for q in range(4):
+                nc.tensor.transpose(bank[:, q * P : (q + 1) * P], blocks[q], ident[:])
+            regrouped = bank[:].rearrange("p (g u r) -> p g r u", g=2, u=2)
+            words = grouped.bitcast(F32).rearrange("p (g r u) -> p g r u", g=2, u=2)
+            if on_vector:
+                nc.vector.tensor_copy(out=words, in_=regrouped)
+            else:
+                nc.scalar.copy(out=words, in_=regrouped)
+
+        def blocks_of(unit):
+            words = raws[unit][:].bitcast(F32)
+            return [
+                words[:, 2 * P * g + u : 2 * P * (g + 1) : 2]
+                for g in range(CHUNK_PASSES)
+                for u in range(2)
+            ]
+
+        def transpose_x(c, t, h):
+            blocks = blocks_of(("x", c, t))[4 * X_BANKS * h : 4 * X_BANKS * (h + 1)]
+            x_grouped = stage.tile([P, STEP_K], BF16, align_bytes=64)
+            for b in range(X_BANKS):
+                transpose_bank(
+                    blocks[4 * b : 4 * b + 4], x_grouped[:, b * K_BANK : (b + 1) * K_BANK], False
+                )
+            return x_grouped
+
+        def transpose_w(c, n):
+            j, b = divmod(n, UNIT_BANKS)
+            w_grouped = stage.tile([P, K_BANK], BF16, align_bytes=64)
+            transpose_bank(blocks_of(("w", c, j))[4 * b : 4 * b + 4], w_grouped[:], n % 2 == 1)
+            return w_grouped
+
+        w_codes = {}
+        w_scales = {}
+
+        def quantise_w(c, n, w_grouped):
+            j, b = divmod(n, UNIT_BANKS)
+            for g in range(2):
+                first = ((2 * b + g) * W_TILES + j) * P
+                nc.vector.quantize_mx(
+                    out=w_codes[c][:, first : first + P].bitcast(FP8X4),
+                    scales=w_scales[c][:, first : first + P],
+                    in_=w_grouped[:, g * 4 * P : (g + 1) * 4 * P],
+                )
+
+        def quantise_x(x_grouped):
+            x_codes = stage.tile([P, STEP_K // 4], U32, align_bytes=64)
+            x_scales = stage.tile([P, STEP_K // 4], U8, align_bytes=64)
+            nc.vector.quantize_mx(out=x_codes[:].bitcast(FP8X4), scales=x_scales[:], in_=x_grouped[:])
+            return x_codes, x_scales
+
+        def multiply(c, t, h, x_codes, x_scales):
+            for g in range(STEP_PASSES):
+                g_chunk = h * STEP_PASSES + g
+                nc.tensor.matmul_mx(
+                    out=acc[t][:],
+                    lhsT=x_codes[:, g * P : (g + 1) * P].bitcast(FP8X4),
+                    lhsT_scale=x_scales[:, g * P : (g + 1) * P],
+                    rhs=w_codes[c][:, g_chunk * H : (g_chunk + 1) * H].bitcast(FP8X4),
+                    rhs_scale=w_scales[c][:, g_chunk * H : (g_chunk + 1) * H],
+                    start=(c == 0 and g_chunk == 0),
+                    stop=(c == n_chunks - 1 and g_chunk == CHUNK_PASSES - 1),
+                )
+
+        def blend_and_store(t):
+            cols = slice(t * H, (t + 1) * H)
+            result = out_pool.tile([P, H], F32, tag="result")
+            nc.vector.tensor_tensor(out=result[:], in0=acc[t][:], in1=gain[:, cols], op=ALU.mult)
+            nc.vector.tensor_tensor(out=result[:], in0=result[:], in1=keep[:, cols], op=ALU.add)
+            nc.sync.dma_start(out=out_rows[t], in_=result[:])
+
+        def new_w_tiles(c):
+            codes = w_pool.tile([P, CHUNK_PASSES * H], U32, align_bytes=64, tag="w_codes")
+            scales = w_pool.tile([P, CHUNK_PASSES * H], U8, align_bytes=64, tag="w_scales")
+            w_codes[c] = codes
+            w_scales[c] = scales
+
+        new_w_tiles(0)
+        w_waiting = []
+        for n in range(W_TILES * UNIT_BANKS):
+            w_now = [(0, n, transpose_w(0, n))]
+            for item in w_waiting:
+                quantise_w(*item)
+            w_waiting = w_now
+
+        n_loaded = RAW_BUFS
+        x_waiting = None
+        x_ready = {}
+        for s in range(n_steps + LAG):
+            if x_waiting is not None:
+                x_ready[s - 1] = quantise_x(x_waiting)
+                x_waiting = None
+            for item in w_waiting:
+                quantise_w(*item)
+            w_waiting = []
+
+            if s < n_steps:
+                c, t, h = steps[s]
+                x_waiting = transpose_x(c, t, h)
+                if c + 1 < n_chunks:
+                    m = t * STEPS_PER_UNIT + h
+                    if m == 0:
+                        new_w_tiles(c + 1)
+                    for n in range(m * W_BANKS, (m + 1) * W_BANKS):
+                        w_waiting.append((c + 1, n, transpose_w(c + 1, n)))
+                if t % 2 == 1 and h == STEPS_PER_UNIT - 1:
+                    n_free = min(len(stream), position[("x", c, t)] + 1 + RAW_BUFS)
+                    for n in range(n_loaded, n_free):
+                        raws[stream[n]] = load(stream[n])
+                    n_loaded = max(n_loaded, n_free)
+
+            if s >= LAG:
+                c_old, t_old, h_old = steps[s - LAG]
+                multiply(c_old, t_old, h_old, *x_ready[s - LAG])
+
+            if s < n_steps and h == 0:
+                prepare_blend(c, t)
+            if s >= LAG and c_old == n_chunks - 1 and h_old == STEPS_PER_UNIT - 1:
+                blend_and_store(t_old)

@@ -15,19 +15,15 @@ ACT = mybir.ActivationFunctionType
 
 P = 128
 K_PASS = 512
-K_BLOCK = 256
 BANK = 512
-K_BANK = 4 * K_BLOCK
-CHUNK = 4096
-UNIT_BANKS = CHUNK // K_BANK
-CHUNK_PASSES = CHUNK // K_PASS
-STEP_K = 2048
-STEP_PASSES = STEP_K // K_PASS
-X_BANKS = STEP_K // K_BANK
-W_BANKS = X_BANKS // 2
-STEPS_PER_UNIT = CHUNK // STEP_K
+K_BANK = 1024
+SLAB = 2048
+SLAB_PASSES = SLAB // K_PASS
+SLAB_BANKS = SLAB // K_BANK
+HALF_RUN = 16
 LAG = 2
-RAW_BUFS = 12
+RAW_BUFS = 28
+FIRST_LOADS = 14
 
 
 def tile_persistentgrucell_pb_k_kernel(
@@ -47,28 +43,22 @@ def tile_persistentgrucell_pb_k_kernel(
     B, I = x.shape
     H = rh.shape[1]
     K = I + H
-    ROW_TILES = B // P
-    W_TILES = H // P
-    n_chunks = K // CHUNK
-    assert n_chunks > 3
-    assert ROW_TILES * STEPS_PER_UNIT * W_BANKS == W_TILES * UNIT_BANKS
+    T = B // P
+    WT = H // P
+    n_slabs = K // SLAB
 
-    x_rows = x.rearrange("(p t) k -> t p k", t=ROW_TILES)
-    rh_rows = rh.rearrange("(p t) c -> t p c", t=ROW_TILES)
-    out_rows = out.rearrange("(p t) h -> t p h", t=ROW_TILES)
+    x_rows = x.rearrange("(p t) k -> t p k", t=T)
+    rh_rows = rh.rearrange("(p t) k -> t p k", t=T)
+    out_rows = out.rearrange("(p t) h -> t p h", t=T)
 
-    stream = [("w", 0, j) for j in range(W_TILES)]
-    for c in range(n_chunks):
-        for j in range(W_TILES):
-            if c + 1 < n_chunks:
-                stream.append(("w", c + 1, j))
-            stream.extend([("x", c, t) for t in range(2 * j, 2 * j + 2)])
-    position = dict([(unit, n) for n, unit in enumerate(stream)])
+    stream = [("w", 0, j) for j in range(WT)]
+    for c in range(n_slabs):
+        for t in range(T):
+            stream.append(("x", c, t))
+            if c + 1 < n_slabs and t < WT:
+                stream.append(("w", c + 1, t))
 
-    steps = []
-    for c in range(n_chunks):
-        for t in range(ROW_TILES):
-            steps.extend([(c, t, h) for h in range(STEPS_PER_UNIT)])
+    steps = [(c, t) for c in range(n_slabs) for t in range(T)]
     n_steps = len(steps)
 
     with ExitStack() as ctx:
@@ -81,194 +71,247 @@ def tile_persistentgrucell_pb_k_kernel(
         acc_pool = ctx.enter_context(tc.psum_pool(name="acc", bufs=1))
         bank_pool = ctx.enter_context(tc.psum_pool(name="banks", bufs=4))
 
+        raws = {}
+
         def load(unit):
             kind, c, r = unit
-            raw = raw_pool.tile([P, CHUNK], BF16, tag="raw")
-            k0 = c * CHUNK
+            raw = raw_pool.tile([P, SLAB], BF16, tag="raw")
+            raws[unit] = raw
+            k0 = c * SLAB
             if kind == "w":
-                nc.sync.dma_start(out=raw[:], in_=Wn[r * P : (r + 1) * P, k0 : k0 + CHUNK])
+                nc.sync.dma_start(out=raw[:], in_=Wn[r * P : (r + 1) * P, k0 : k0 + SLAB])
             else:
-                width = min(CHUNK, I - k0)
+                width = min(SLAB, I - k0)
                 nc.sync.dma_start(out=raw[:, 0:width], in_=x_rows[r][:, k0 : k0 + width])
-                if width < CHUNK:
-                    nc.sync.dma_start(out=raw[:, width:CHUNK], in_=rh_rows[r])
-            return raw
+                if width < SLAB:
+                    nc.sync.dma_start(out=raw[:, width:SLAB], in_=rh_rows[r])
+
+        for j in range(WT):
+            raws[("w", 0, j)] = raw_pool.tile([P, SLAB], BF16, name="raw", tag="raw")
+        for b in range(SLAB_BANKS):
+            for j in range(WT):
+                cols = slice(b * K_BANK, (b + 1) * K_BANK)
+                nc.sync.dma_start(
+                    out=raws[("w", 0, j)][:, cols], in_=Wn[j * P : (j + 1) * P, cols]
+                )
+        n_loaded = WT
+        while n_loaded < FIRST_LOADS:
+            load(stream[n_loaded])
+            n_loaded += 1
 
         ident = const.tile([P, P], F32)
         make_identity(nc, ident[:])
         ones = const.tile([P, P], BF16)
         nc.vector.memset(ones[:], 1.0)
         vectors = const.tile([P, 2 * BANK], BF16)
-        nc.vector.memset(vectors[:], 0.0)
+        nc.gpsimd.memset(vectors[:], 0.0)
         zero = const.tile([P, 1], F32)
         nc.vector.memset(zero[:], 0.0)
-
-        raws = {}
-        for i in range(2):
-            raws[stream[i]] = load(stream[i])
-        hid = const.tile([P, ROW_TILES * H], BF16)
-        nc.scalar.dma_start(out=hid[:], in_=hidden.rearrange("(p t) h -> p (t h)", t=ROW_TILES))
-        nc.scalar.dma_start(out=vectors[0:1, 0:H], in_=bn.unsqueeze(0))
-        nc.scalar.dma_start(out=vectors[0:1, H : 2 * H], in_=connection_strength.unsqueeze(0))
-        nc.scalar.dma_start(out=vectors[0:1, BANK : BANK + H], in_=connection_history.unsqueeze(0))
-        nc.scalar.dma_start(
-            out=vectors[0:1, BANK + H : BANK + H + 1], in_=connection_decay.unsqueeze(0)
-        )
-        upd = const.tile([P, ROW_TILES * H], BF16)
-        nc.scalar.dma_start(out=upd[:], in_=update.rearrange("(p t) h -> p (t h)", t=ROW_TILES))
-        for i in range(2, RAW_BUFS):
-            raws[stream[i]] = load(stream[i])
-
         warm = const.tile([P, 1], F32)
         nc.scalar.activation(out=warm[:], in_=zero[:], func=ACT.Sigmoid)
 
-        habs = const.tile([P, ROW_TILES * H], BF16)
-        nc.vector.scalar_tensor_tensor(
-            out=habs[:], in0=hid[:], scalar=-1.0, in1=hid[:], op0=ALU.mult, op1=ALU.max
-        )
-        spread_a = acc_pool.tile([P, BANK], F32, tag="acc0")
-        nc.tensor.matmul(spread_a[:], lhsT=ones[:], rhs=vectors[:, 0:BANK], start=True, stop=True)
-        spread_b = acc_pool.tile([P, BANK], F32, tag="acc1")
-        nc.tensor.matmul(
-            spread_b[:], lhsT=ones[:], rhs=vectors[:, BANK : 2 * BANK], start=True, stop=True
-        )
-        abs_sum = acc_pool.tile([P, H], F32, tag="acc2")
-        for t in range(ROW_TILES):
-            nc.tensor.matmul(
-                abs_sum[:],
-                lhsT=ones[:],
-                rhs=habs[:, t * H : (t + 1) * H],
-                start=(t == 0),
-                stop=(t == ROW_TILES - 1),
+        hid = const.tile([P, T * H], BF16)
+        upd = const.tile([P, T * H], BF16)
+
+        def load_small():
+            nc.sync.dma_start(out=hid[:], in_=hidden.rearrange("(p t) h -> p (t h)", t=T))
+            nc.sync.dma_start(out=upd[:], in_=update.rearrange("(p t) h -> p (t h)", t=T))
+            nc.sync.dma_start(out=vectors[0:1, 0:H], in_=bn.unsqueeze(0))
+            nc.sync.dma_start(out=vectors[0:1, H : 2 * H], in_=connection_strength.unsqueeze(0))
+            nc.sync.dma_start(out=vectors[0:1, BANK : BANK + H], in_=connection_history.unsqueeze(0))
+            nc.sync.dma_start(
+                out=vectors[0:1, BANK + H : BANK + H + 1], in_=connection_decay.unsqueeze(0)
             )
-        keep = const.tile([P, ROW_TILES * H], F32)
-        nc.vector.tensor_tensor(out=keep[:], in0=upd[:], in1=hid[:], op=ALU.mult)
-        nc.vector.tensor_tensor(out=keep[:], in0=hid[:], in1=keep[:], op=ALU.subtract)
-        decay = const.tile([P, 1], F32)
-        nc.vector.tensor_copy(out=decay[:], in_=spread_b[:, H : H + 1])
-        ch = const.tile([P, H], F32)
-        nc.vector.tensor_scalar(
-            out=ch[:], in0=spread_b[:, 0:H], scalar1=decay[:, 0:1], scalar2=None, op0=ALU.mult
-        )
-        nc.vector.scalar_tensor_tensor(
-            out=ch[:], in0=abs_sum[:], scalar=1.0 / B, in1=ch[:], op0=ALU.mult, op1=ALU.add
-        )
-        sig = const.tile([P, H], F32)
-        nc.scalar.activation(out=sig[:], in_=ch[:], func=ACT.Sigmoid)
+
+        load_small()
+        while n_loaded < RAW_BUFS:
+            load(stream[n_loaded])
+            n_loaded += 1
+
+        habs = const.tile([P, T * H], BF16)
         cs = const.tile([P, H], F32)
-        nc.vector.tensor_tensor(out=cs[:], in0=sig[:], in1=spread_a[:, H : 2 * H], op=ALU.mult)
         cs_bn = const.tile([P, H], F32)
-        nc.vector.tensor_tensor(out=cs_bn[:], in0=cs[:], in1=spread_a[:, 0:H], op=ALU.mult)
+        ch = const.tile([P, H], F32)
+        decay = const.tile([P, 1], F32)
+        sig = const.tile([P, H], F32)
+        gain = const.tile([P, T * H], F32)
+        keep = const.tile([P, T * H], F32)
 
-        gain = const.tile([P, ROW_TILES * H], F32)
-        bias = const.tile([P, ROW_TILES * H], F32)
+        def spread(cols):
+            bank = bank_pool.tile([P, BANK], F32, tag="bank")
+            nc.tensor.matmul(bank[:], lhsT=ones[:], rhs=vectors[:, cols], start=True, stop=True)
+            return bank
 
-        def prepare_blend(step, t):
+        def task_abs():
+            nc.vector.scalar_tensor_tensor(
+                out=habs[:], in0=hid[:], scalar=-1.0, in1=hid[:], op0=ALU.mult, op1=ALU.max
+            )
+
+        def task_history():
+            bank = spread(slice(BANK, 2 * BANK))
+            nc.vector.tensor_copy(out=decay[:], in_=bank[:, H : H + 1])
+            nc.vector.tensor_scalar(
+                out=ch[:], in0=bank[:, 0:H], scalar1=decay[:, 0:1], scalar2=None, op0=ALU.mult
+            )
+
+        def task_mean():
+            bank = bank_pool.tile([P, BANK], F32, tag="bank")
+            for t in range(T):
+                nc.tensor.matmul(
+                    bank[:, 0:H],
+                    lhsT=ones[:],
+                    rhs=habs[:, t * H : (t + 1) * H],
+                    start=(t == 0),
+                    stop=(t == T - 1),
+                )
+            nc.vector.scalar_tensor_tensor(
+                out=ch[:], in0=bank[:, 0:H], scalar=1.0 / B, in1=ch[:], op0=ALU.mult, op1=ALU.add
+            )
+            nc.scalar.activation(out=sig[:], in_=ch[:], func=ACT.Sigmoid)
+
+        def task_strength():
+            bank = spread(slice(0, BANK))
+            nc.vector.tensor_tensor(out=cs[:], in0=sig[:], in1=bank[:, H : 2 * H], op=ALU.mult)
+            nc.vector.tensor_tensor(out=cs_bn[:], in0=cs[:], in1=bank[:, 0:H], op=ALU.mult)
+
+        def task_blend(t, part):
             cols = slice(t * H, (t + 1) * H)
-            if step == 0:
+            if part == 0:
                 nc.vector.tensor_tensor(out=gain[:, cols], in0=upd[:, cols], in1=cs[:], op=ALU.mult)
-            elif step == 1:
-                nc.vector.tensor_tensor(out=bias[:, cols], in0=upd[:, cols], in1=cs_bn[:], op=ALU.mult)
-            elif step == 2:
                 nc.vector.tensor_tensor(
-                    out=keep[:, cols], in0=keep[:, cols], in1=bias[:, cols], op=ALU.add
+                    out=keep[:, cols], in0=cs_bn[:], in1=hid[:, cols], op=ALU.subtract
+                )
+            elif part == 1:
+                nc.vector.tensor_tensor(
+                    out=keep[:, cols], in0=upd[:, cols], in1=keep[:, cols], op=ALU.mult
+                )
+            else:
+                nc.vector.tensor_tensor(
+                    out=keep[:, cols], in0=hid[:, cols], in1=keep[:, cols], op=ALU.add
                 )
 
+        tasks = [task_abs, task_history, task_mean, task_strength]
+        for part in range(3):
+            for t in range(T):
+                tasks.append((lambda t, part: lambda: task_blend(t, part))(t, part))
+        FIRST_TASK = n_steps - len(tasks) - 4
+
         acc = [
-            acc_pool.tile([P, H], F32, name="acc%d" % t, tag="acc%d" % t) for t in range(ROW_TILES)
+            acc_pool.tile([P, BANK], F32, name="acc%d" % t, tag="acc%d" % t) for t in range(T)
         ]
 
-        def transpose_bank(blocks, grouped, on_vector):
+        def transpose_bank(blocks, words_out):
             bank = bank_pool.tile([P, BANK], F32, tag="bank")
             for q in range(4):
                 nc.tensor.transpose(bank[:, q * P : (q + 1) * P], blocks[q], ident[:])
             regrouped = bank[:].rearrange("p (g u r) -> p g r u", g=2, u=2)
-            words = grouped.bitcast(F32).rearrange("p (g r u) -> p g r u", g=2, u=2)
-            if on_vector:
-                nc.vector.tensor_copy(out=words, in_=regrouped)
-            else:
-                nc.scalar.copy(out=words, in_=regrouped)
+            nc.scalar.copy(out=words_out, in_=regrouped)
 
-        def blocks_of(unit):
-            words = raws[unit][:].bitcast(F32)
+        def split_halves(unit, first_bank, n_banks):
+            n = n_banks * K_BANK
+            split = stage.tile([P, n], BF16, name="split%d" % n_banks, tag="split%d" % n_banks)
+            source = raws[unit][:, first_bank * K_BANK : first_bank * K_BANK + n]
+            nc.vector.tensor_copy(
+                out=split[:].rearrange("p (u b e) -> p u b e", u=2, e=HALF_RUN),
+                in_=source.rearrange("p (b u e) -> p u b e", u=2, e=HALF_RUN),
+            )
+            return split
+
+        def split_blocks(split, n_banks):
+            words = split[:].bitcast(F32)
+            half = n_banks * K_BANK // 4
             return [
-                words[:, 2 * P * g + u : 2 * P * (g + 1) : 2]
-                for g in range(CHUNK_PASSES)
+                words[:, u * half + g * P : u * half + (g + 1) * P]
+                for g in range(2 * n_banks)
                 for u in range(2)
             ]
 
-        def transpose_x(c, t, h):
-            blocks = blocks_of(("x", c, t))[4 * X_BANKS * h : 4 * X_BANKS * (h + 1)]
-            x_grouped = stage.tile([P, STEP_K], BF16, align_bytes=64)
-            for b in range(X_BANKS):
-                transpose_bank(
-                    blocks[4 * b : 4 * b + 4], x_grouped[:, b * K_BANK : (b + 1) * K_BANK], False
-                )
-            return x_grouped
+        def transpose_x(blocks):
+            grouped = stage.tile([P, SLAB], BF16, name="x_grouped", align_bytes=64, tag="x_grouped")
+            words = grouped[:].bitcast(F32).rearrange("p (g r u) -> p g r u", r=P, u=2)
+            for b in range(SLAB_BANKS):
+                transpose_bank(blocks[4 * b : 4 * b + 4], words[:, 2 * b : 2 * b + 2])
+            return grouped
 
-        def transpose_w(c, n):
-            j, b = divmod(n, UNIT_BANKS)
-            w_grouped = stage.tile([P, K_BANK], BF16, align_bytes=64)
-            transpose_bank(blocks_of(("w", c, j))[4 * b : 4 * b + 4], w_grouped[:], n % 2 == 1)
-            return w_grouped
+        w_grouped = {}
+
+        def transpose_w(c, j, b, blocks):
+            if (c, b) not in w_grouped:
+                grouped = w_pool.tile(
+                    [P, 2 * WT * P * 4], BF16, name="w_grouped", align_bytes=64, tag="w_grouped"
+                )
+                w_grouped[(c, b)] = grouped
+            words = w_grouped[(c, b)][:].bitcast(F32)
+            words = words.rearrange("p (g j r u) -> p j g r u", j=WT, r=P, u=2)
+            transpose_bank(blocks, words[:, j])
 
         w_codes = {}
         w_scales = {}
 
-        def quantise_w(c, n, w_grouped):
-            j, b = divmod(n, UNIT_BANKS)
-            for g in range(2):
-                first = ((2 * b + g) * W_TILES + j) * P
-                nc.vector.quantize_mx(
-                    out=w_codes[c][:, first : first + P].bitcast(FP8X4),
-                    scales=w_scales[c][:, first : first + P],
-                    in_=w_grouped[:, g * 4 * P : (g + 1) * 4 * P],
-                )
+        def new_w_tiles(c):
+            codes = w_pool.tile([P, SLAB_PASSES * H], U32, align_bytes=64, tag="w_codes")
+            scales = w_pool.tile([P, SLAB_PASSES * H], U8, align_bytes=64, tag="w_scales")
+            w_codes[c] = codes
+            w_scales[c] = scales
 
-        def quantise_x(x_grouped):
-            x_codes = stage.tile([P, STEP_K // 4], U32, align_bytes=64)
-            x_scales = stage.tile([P, STEP_K // 4], U8, align_bytes=64)
-            nc.vector.quantize_mx(out=x_codes[:].bitcast(FP8X4), scales=x_scales[:], in_=x_grouped[:])
-            return x_codes, x_scales
+        def quantise_w(c, b):
+            cols = slice(b * 2 * H, (b + 1) * 2 * H)
+            nc.vector.quantize_mx(
+                out=w_codes[c][:, cols].bitcast(FP8X4),
+                scales=w_scales[c][:, cols],
+                in_=w_grouped[(c, b)][:],
+            )
 
-        def multiply(c, t, h, x_codes, x_scales):
-            for g in range(STEP_PASSES):
-                g_chunk = h * STEP_PASSES + g
+        def quantise_x(grouped):
+            codes = stage.tile([P, SLAB // 4], U32, align_bytes=64)
+            scales = stage.tile([P, SLAB // 4], U8, align_bytes=64)
+            nc.vector.quantize_mx(out=codes[:].bitcast(FP8X4), scales=scales[:], in_=grouped[:])
+            return codes, scales
+
+        def multiply(c, t, codes, scales):
+            for g in range(SLAB_PASSES):
                 nc.tensor.matmul_mx(
-                    out=acc[t][:],
-                    lhsT=x_codes[:, g * P : (g + 1) * P].bitcast(FP8X4),
-                    lhsT_scale=x_scales[:, g * P : (g + 1) * P],
-                    rhs=w_codes[c][:, g_chunk * H : (g_chunk + 1) * H].bitcast(FP8X4),
-                    rhs_scale=w_scales[c][:, g_chunk * H : (g_chunk + 1) * H],
-                    start=(c == 0 and g_chunk == 0),
-                    stop=(c == n_chunks - 1 and g_chunk == CHUNK_PASSES - 1),
+                    out=acc[t][:, 0:H],
+                    lhsT=codes[:, g * P : (g + 1) * P].bitcast(FP8X4),
+                    lhsT_scale=scales[:, g * P : (g + 1) * P],
+                    rhs=w_codes[c][:, g * H : (g + 1) * H].bitcast(FP8X4),
+                    rhs_scale=w_scales[c][:, g * H : (g + 1) * H],
+                    start=(c == 0 and g == 0),
+                    stop=(c == n_slabs - 1 and g == SLAB_PASSES - 1),
                 )
 
         def blend_and_store(t):
             cols = slice(t * H, (t + 1) * H)
             result = out_pool.tile([P, H], F32, tag="result")
-            nc.vector.tensor_tensor(out=result[:], in0=acc[t][:], in1=gain[:, cols], op=ALU.mult)
+            nc.vector.tensor_tensor(out=result[:], in0=acc[t][:, 0:H], in1=gain[:, cols], op=ALU.mult)
             nc.vector.tensor_tensor(out=result[:], in0=result[:], in1=keep[:, cols], op=ALU.add)
             nc.sync.dma_start(out=out_rows[t], in_=result[:])
 
-        def new_w_tiles(c):
-            codes = w_pool.tile([P, CHUNK_PASSES * H], U32, align_bytes=64, tag="w_codes")
-            scales = w_pool.tile([P, CHUNK_PASSES * H], U8, align_bytes=64, tag="w_scales")
-            w_codes[c] = codes
-            w_scales[c] = scales
-
         new_w_tiles(0)
-        w_waiting = []
-        for n in range(W_TILES * UNIT_BANKS):
-            w_now = [(0, n, transpose_w(0, n))]
-            for item in w_waiting:
-                quantise_w(*item)
-            w_waiting = w_now
+        for b in range(SLAB_BANKS):
+            for j in range(WT):
+                transpose_w(0, j, b, split_blocks(split_halves(("w", 0, j), b, 1), 1))
 
-        n_loaded = RAW_BUFS
+        w_waiting = [(0, b) for b in range(SLAB_BANKS)]
         x_waiting = None
         x_ready = {}
+        x_split = {}
+        w_split = {}
+
+        def w_bank_of(s):
+            c, m = steps[s]
+            return (c + 1, m % WT, m // WT)
+
         for s in range(n_steps + LAG):
+            if s == 0:
+                x_split[0] = split_halves(("x", 0, 0), 0, SLAB_BANKS)
+                w_split[0] = split_halves(("w", 1, 0), 0, 1)
+            if s + 1 < n_steps:
+                c, t = steps[s + 1]
+                x_split[s + 1] = split_halves(("x", c, t), 0, SLAB_BANKS)
+                cw, j, b = w_bank_of(s + 1)
+                if cw < n_slabs:
+                    w_split[s + 1] = split_halves(("w", cw, j), b, 1)
             if x_waiting is not None:
                 x_ready[s - 1] = quantise_x(x_waiting)
                 x_waiting = None
@@ -277,25 +320,25 @@ def tile_persistentgrucell_pb_k_kernel(
             w_waiting = []
 
             if s < n_steps:
-                c, t, h = steps[s]
-                x_waiting = transpose_x(c, t, h)
-                if c + 1 < n_chunks:
-                    m = t * STEPS_PER_UNIT + h
-                    if m == 0:
-                        new_w_tiles(c + 1)
-                    for n in range(m * W_BANKS, (m + 1) * W_BANKS):
-                        w_waiting.append((c + 1, n, transpose_w(c + 1, n)))
-                if t % 2 == 1 and h == STEPS_PER_UNIT - 1:
-                    n_free = min(len(stream), position[("x", c, t)] + 1 + RAW_BUFS)
-                    for n in range(n_loaded, n_free):
-                        raws[stream[n]] = load(stream[n])
-                    n_loaded = max(n_loaded, n_free)
+                x_waiting = transpose_x(split_blocks(x_split[s], SLAB_BANKS))
+                c, t = steps[s]
+                cw, j, b = w_bank_of(s)
+                if cw < n_slabs:
+                    if (j, b) == (0, 0):
+                        new_w_tiles(cw)
+                    transpose_w(cw, j, b, split_blocks(w_split[s], 1))
+                    if j == WT - 1:
+                        w_waiting.append((cw, b))
+                if t == T - 1:
+                    n_free = min(len(stream), stream.index(("x", c, t)) + 1 + RAW_BUFS)
+                    while n_loaded < n_free:
+                        load(stream[n_loaded])
+                        n_loaded += 1
 
             if s >= LAG:
-                c_old, t_old, h_old = steps[s - LAG]
-                multiply(c_old, t_old, h_old, *x_ready[s - LAG])
-
-            if s < n_steps and h == 0:
-                prepare_blend(c, t)
-            if s >= LAG and c_old == n_chunks - 1 and h_old == STEPS_PER_UNIT - 1:
+                c_old, t_old = steps[s - LAG]
+                multiply(c_old, t_old, *x_ready[s - LAG])
+            if 0 <= s - FIRST_TASK < len(tasks):
+                tasks[s - FIRST_TASK]()
+            if s >= LAG and c_old == n_slabs - 1:
                 blend_and_store(t_old)

@@ -20,6 +20,7 @@ K_BANK = 1024
 SLAB = 2048
 SLAB_PASSES = SLAB // K_PASS
 SLAB_BANKS = SLAB // K_BANK
+SPLIT_BANKS = (1,)
 HALF_RUN = 16
 LAG = 2
 RAW_BUFS = 28
@@ -207,30 +208,39 @@ def tile_persistentgrucell_pb_k_kernel(
             regrouped = bank[:].rearrange("p (g u r) -> p g r u", g=2, u=2)
             nc.scalar.copy(out=words_out, in_=regrouped)
 
-        def split_halves(unit, first_bank, n_banks):
-            n = n_banks * K_BANK
-            split = stage.tile([P, n], BF16, name="split%d" % n_banks, tag="split%d" % n_banks)
-            source = raws[unit][:, first_bank * K_BANK : first_bank * K_BANK + n]
+        def split_halves(unit, b):
+            if b not in SPLIT_BANKS:
+                return None
+            tag = "split_" + unit[0]
+            split = stage.tile([P, K_BANK], BF16, name=tag, tag=tag)
+            source = raws[unit][:, b * K_BANK : (b + 1) * K_BANK]
             nc.vector.tensor_copy(
                 out=split[:].rearrange("p (u b e) -> p u b e", u=2, e=HALF_RUN),
                 in_=source.rearrange("p (b u e) -> p u b e", u=2, e=HALF_RUN),
             )
             return split
 
-        def split_blocks(split, n_banks):
-            words = split[:].bitcast(F32)
-            half = n_banks * K_BANK // 4
+        def bank_blocks(unit, b, split):
+            if split is not None:
+                words = split[:].bitcast(F32)
+                half = K_BANK // 4
+                return [
+                    words[:, u * half + g * P : u * half + (g + 1) * P]
+                    for g in range(2)
+                    for u in range(2)
+                ]
+            words = raws[unit][:].bitcast(F32)
             return [
-                words[:, u * half + g * P : u * half + (g + 1) * P]
-                for g in range(2 * n_banks)
+                words[:, 2 * P * g + u : 2 * P * (g + 1) : 2]
+                for g in range(2 * b, 2 * b + 2)
                 for u in range(2)
             ]
 
-        def transpose_x(blocks):
+        def transpose_x(unit, splits):
             grouped = stage.tile([P, SLAB], BF16, name="x_grouped", align_bytes=64, tag="x_grouped")
             words = grouped[:].bitcast(F32).rearrange("p (g r u) -> p g r u", r=P, u=2)
             for b in range(SLAB_BANKS):
-                transpose_bank(blocks[4 * b : 4 * b + 4], words[:, 2 * b : 2 * b + 2])
+                transpose_bank(bank_blocks(unit, b, splits[b]), words[:, 2 * b : 2 * b + 2])
             return grouped
 
         w_grouped = {}
@@ -290,7 +300,8 @@ def tile_persistentgrucell_pb_k_kernel(
         new_w_tiles(0)
         for b in range(SLAB_BANKS):
             for j in range(WT):
-                transpose_w(0, j, b, split_blocks(split_halves(("w", 0, j), b, 1), 1))
+                unit = ("w", 0, j)
+                transpose_w(0, j, b, bank_blocks(unit, b, split_halves(unit, b)))
 
         w_waiting = [(0, b) for b in range(SLAB_BANKS)]
         x_waiting = None
@@ -304,14 +315,14 @@ def tile_persistentgrucell_pb_k_kernel(
 
         for s in range(n_steps + LAG):
             if s == 0:
-                x_split[0] = split_halves(("x", 0, 0), 0, SLAB_BANKS)
-                w_split[0] = split_halves(("w", 1, 0), 0, 1)
+                x_split[0] = [split_halves(("x", 0, 0), b) for b in range(SLAB_BANKS)]
+                w_split[0] = split_halves(("w", 1, 0), 0)
             if s + 1 < n_steps:
                 c, t = steps[s + 1]
-                x_split[s + 1] = split_halves(("x", c, t), 0, SLAB_BANKS)
+                x_split[s + 1] = [split_halves(("x", c, t), b) for b in range(SLAB_BANKS)]
                 cw, j, b = w_bank_of(s + 1)
                 if cw < n_slabs:
-                    w_split[s + 1] = split_halves(("w", cw, j), b, 1)
+                    w_split[s + 1] = split_halves(("w", cw, j), b)
             if x_waiting is not None:
                 x_ready[s - 1] = quantise_x(x_waiting)
                 x_waiting = None
@@ -320,13 +331,13 @@ def tile_persistentgrucell_pb_k_kernel(
             w_waiting = []
 
             if s < n_steps:
-                x_waiting = transpose_x(split_blocks(x_split[s], SLAB_BANKS))
+                x_waiting = transpose_x(("x",) + steps[s], x_split[s])
                 c, t = steps[s]
                 cw, j, b = w_bank_of(s)
                 if cw < n_slabs:
                     if (j, b) == (0, 0):
                         new_w_tiles(cw)
-                    transpose_w(cw, j, b, split_blocks(w_split[s], 1))
+                    transpose_w(cw, j, b, bank_blocks(("w", cw, j), b, w_split[s]))
                     if j == WT - 1:
                         w_waiting.append((cw, b))
                 if t == T - 1:

@@ -20,7 +20,7 @@ K_BANK = 1024
 SLAB = 2048
 SLAB_PASSES = SLAB // K_PASS
 SLAB_BANKS = SLAB // K_BANK
-SPLIT_BANKS = (1,)
+FIRST_SPLIT = 1
 HALF_RUN = 16
 LAG = 2
 RAW_BUFS = 28
@@ -208,39 +208,35 @@ def tile_persistentgrucell_pb_k_kernel(
             regrouped = bank[:].rearrange("p (g u r) -> p g r u", g=2, u=2)
             nc.scalar.copy(out=words_out, in_=regrouped)
 
-        def split_halves(unit, b):
-            if b not in SPLIT_BANKS:
-                return None
+        def split_halves(unit, first, last):
+            first = max(first, FIRST_SPLIT)
             tag = "split_" + unit[0]
-            split = stage.tile([P, K_BANK], BF16, name=tag, tag=tag)
-            source = raws[unit][:, b * K_BANK : (b + 1) * K_BANK]
+            split = stage.tile([P, (last - first) * K_PASS], BF16, name=tag, tag=tag)
+            source = raws[unit][:, first * K_PASS : last * K_PASS]
             nc.vector.tensor_copy(
                 out=split[:].rearrange("p (u b e) -> p u b e", u=2, e=HALF_RUN),
                 in_=source.rearrange("p (b u e) -> p u b e", u=2, e=HALF_RUN),
             )
-            return split
+            return split[:].bitcast(F32), first, last
 
         def bank_blocks(unit, b, split):
-            if split is not None:
-                words = split[:].bitcast(F32)
-                half = K_BANK // 4
-                return [
-                    words[:, u * half + g * P : u * half + (g + 1) * P]
-                    for g in range(2)
-                    for u in range(2)
-                ]
-            words = raws[unit][:].bitcast(F32)
-            return [
-                words[:, 2 * P * g + u : 2 * P * (g + 1) : 2]
-                for g in range(2 * b, 2 * b + 2)
-                for u in range(2)
-            ]
+            split_words, first, last = split
+            raw_words = raws[unit][:].bitcast(F32)
+            blocks = []
+            for g in (2 * b, 2 * b + 1):
+                for u in range(2):
+                    if g < FIRST_SPLIT:
+                        blocks.append(raw_words[:, 2 * P * g + u : 2 * P * (g + 1) : 2])
+                    else:
+                        start = (u * (last - first) + g - first) * P
+                        blocks.append(split_words[:, start : start + P])
+            return blocks
 
-        def transpose_x(unit, splits):
+        def transpose_x(unit, split):
             grouped = stage.tile([P, SLAB], BF16, name="x_grouped", align_bytes=64, tag="x_grouped")
             words = grouped[:].bitcast(F32).rearrange("p (g r u) -> p g r u", r=P, u=2)
             for b in range(SLAB_BANKS):
-                transpose_bank(bank_blocks(unit, b, splits[b]), words[:, 2 * b : 2 * b + 2])
+                transpose_bank(bank_blocks(unit, b, split), words[:, 2 * b : 2 * b + 2])
             return grouped
 
         w_grouped = {}
@@ -301,7 +297,7 @@ def tile_persistentgrucell_pb_k_kernel(
         for b in range(SLAB_BANKS):
             for j in range(WT):
                 unit = ("w", 0, j)
-                transpose_w(0, j, b, bank_blocks(unit, b, split_halves(unit, b)))
+                transpose_w(0, j, b, bank_blocks(unit, b, split_halves(unit, 2 * b, 2 * b + 2)))
 
         w_waiting = [(0, b) for b in range(SLAB_BANKS)]
         x_waiting = None
@@ -315,14 +311,14 @@ def tile_persistentgrucell_pb_k_kernel(
 
         for s in range(n_steps + LAG):
             if s == 0:
-                x_split[0] = [split_halves(("x", 0, 0), b) for b in range(SLAB_BANKS)]
-                w_split[0] = split_halves(("w", 1, 0), 0)
+                x_split[0] = split_halves(("x", 0, 0), 0, SLAB_PASSES)
+                w_split[0] = split_halves(("w", 1, 0), 0, 2)
             if s + 1 < n_steps:
                 c, t = steps[s + 1]
-                x_split[s + 1] = [split_halves(("x", c, t), b) for b in range(SLAB_BANKS)]
+                x_split[s + 1] = split_halves(("x", c, t), 0, SLAB_PASSES)
                 cw, j, b = w_bank_of(s + 1)
                 if cw < n_slabs:
-                    w_split[s + 1] = split_halves(("w", cw, j), b)
+                    w_split[s + 1] = split_halves(("w", cw, j), 2 * b, 2 * b + 2)
             if x_waiting is not None:
                 x_ready[s - 1] = quantise_x(x_waiting)
                 x_waiting = None

@@ -21,7 +21,6 @@ SLAB = 2048
 SLAB_PASSES = SLAB // K_PASS
 SLAB_BANKS = SLAB // K_BANK
 FIRST_SPLIT = 1
-HALF_RUN = 16
 LAG = 2
 RAW_BUFS = 28
 FIRST_LOADS = 14
@@ -213,11 +212,12 @@ def tile_persistentgrucell_pb_k_kernel(
             tag = "split_" + unit[0]
             split = stage.tile([P, (last - first) * K_PASS], BF16, name=tag, tag=tag)
             source = raws[unit][:, first * K_PASS : last * K_PASS]
+            words = split[:].bitcast(F32)
             nc.vector.tensor_copy(
-                out=split[:].rearrange("p (u b e) -> p u b e", u=2, e=HALF_RUN),
-                in_=source.rearrange("p (b u e) -> p u b e", u=2, e=HALF_RUN),
+                out=words.rearrange("p (u w) -> p u w", u=2),
+                in_=source.bitcast(F32).rearrange("p (w u) -> p u w", u=2),
             )
-            return split[:].bitcast(F32), first, last
+            return words, first, last
 
         def bank_blocks(unit, b, split):
             split_words, first, last = split

@@ -20,7 +20,8 @@ K_BANK = 1024
 SLAB = 2048
 SLAB_PASSES = SLAB // K_PASS
 SLAB_BANKS = SLAB // K_BANK
-FIRST_SPLIT = 1
+X_FIRST_SPLIT = 1
+W_FIRST_SPLIT = 2
 LAG = 2
 RAW_BUFS = 28
 FIRST_LOADS = 14
@@ -67,11 +68,12 @@ def tile_persistentgrucell_pb_k_kernel(
         raw_pool = ctx.enter_context(tc.tile_pool(name="raw", bufs=RAW_BUFS))
         stage = ctx.enter_context(tc.tile_pool(name="stage", bufs=LAG + 2))
         w_pool = ctx.enter_context(tc.tile_pool(name="wq", bufs=3))
-        out_pool = ctx.enter_context(tc.tile_pool(name="outs", bufs=2))
+        out_pool = ctx.enter_context(tc.tile_pool(name="outs", bufs=T))
         acc_pool = ctx.enter_context(tc.psum_pool(name="acc", bufs=1))
         bank_pool = ctx.enter_context(tc.psum_pool(name="banks", bufs=4))
 
         raws = {}
+        splits = {}
 
         def load(unit):
             kind, c, r = unit
@@ -142,20 +144,24 @@ def tile_persistentgrucell_pb_k_kernel(
             nc.tensor.matmul(bank[:], lhsT=ones[:], rhs=vectors[:, cols], start=True, stop=True)
             return bank
 
-        def task_abs():
-            nc.vector.scalar_tensor_tensor(
-                out=habs[:], in0=hid[:], scalar=-1.0, in1=hid[:], op0=ALU.mult, op1=ALU.max
-            )
+        banks = {}
 
-        def task_history():
-            bank = spread(slice(BANK, 2 * BANK))
+        def abs_hidden():
+            nc.scalar.activation(out=habs[:], in_=hid[:], func=ACT.Abs)
+
+        def spread_history():
+            banks["history"] = spread(slice(BANK, 2 * BANK))
+
+        def use_history():
+            bank = banks["history"]
             nc.vector.tensor_copy(out=decay[:], in_=bank[:, H : H + 1])
             nc.vector.tensor_scalar(
                 out=ch[:], in0=bank[:, 0:H], scalar1=decay[:, 0:1], scalar2=None, op0=ALU.mult
             )
 
-        def task_mean():
+        def sum_hidden():
             bank = bank_pool.tile([P, BANK], F32, tag="bank")
+            banks["mean"] = bank
             for t in range(T):
                 nc.tensor.matmul(
                     bank[:, 0:H],
@@ -164,37 +170,61 @@ def tile_persistentgrucell_pb_k_kernel(
                     start=(t == 0),
                     stop=(t == T - 1),
                 )
+
+        def use_mean():
+            bank = banks["mean"]
             nc.vector.scalar_tensor_tensor(
                 out=ch[:], in0=bank[:, 0:H], scalar=1.0 / B, in1=ch[:], op0=ALU.mult, op1=ALU.add
             )
+
+        def sigmoid():
             nc.scalar.activation(out=sig[:], in_=ch[:], func=ACT.Sigmoid)
 
-        def task_strength():
-            bank = spread(slice(0, BANK))
+        def spread_strength():
+            banks["strength"] = spread(slice(0, BANK))
+
+        def use_strength():
+            bank = banks["strength"]
             nc.vector.tensor_tensor(out=cs[:], in0=sig[:], in1=bank[:, H : 2 * H], op=ALU.mult)
             nc.vector.tensor_tensor(out=cs_bn[:], in0=cs[:], in1=bank[:, 0:H], op=ALU.mult)
 
-        def task_blend(t, part):
-            cols = slice(t * H, (t + 1) * H)
-            if part == 0:
-                nc.vector.tensor_tensor(out=gain[:, cols], in0=upd[:, cols], in1=cs[:], op=ALU.mult)
-                nc.vector.tensor_tensor(
-                    out=keep[:, cols], in0=cs_bn[:], in1=hid[:, cols], op=ALU.subtract
-                )
-            elif part == 1:
-                nc.vector.tensor_tensor(
-                    out=keep[:, cols], in0=upd[:, cols], in1=keep[:, cols], op=ALU.mult
-                )
-            else:
-                nc.vector.tensor_tensor(
-                    out=keep[:, cols], in0=hid[:, cols], in1=keep[:, cols], op=ALU.add
-                )
+        def rows_of(tile, first):
+            return tile[:, first * H : (first + 2) * H].rearrange("p (t h) -> p t h", t=2)
 
-        tasks = [task_abs, task_history, task_mean, task_strength]
-        for part in range(3):
-            for t in range(T):
-                tasks.append((lambda t, part: lambda: task_blend(t, part))(t, part))
-        FIRST_TASK = n_steps - len(tasks) - 4
+        def both(tile):
+            return tile[:].unsqueeze(1).to_broadcast([P, 2, H])
+
+        def make_gain(first):
+            nc.vector.tensor_tensor(
+                out=rows_of(gain, first), in0=rows_of(upd, first), in1=both(cs), op=ALU.mult
+            )
+
+        def keep_difference(first):
+            nc.vector.tensor_tensor(
+                out=rows_of(keep, first), in0=both(cs_bn), in1=rows_of(hid, first), op=ALU.subtract
+            )
+
+        def keep_product(first):
+            nc.vector.tensor_tensor(
+                out=rows_of(keep, first), in0=rows_of(upd, first), in1=rows_of(keep, first), op=ALU.mult
+            )
+
+        def keep_sum(first):
+            nc.vector.tensor_tensor(
+                out=rows_of(keep, first), in0=rows_of(hid, first), in1=rows_of(keep, first), op=ALU.add
+            )
+
+        tasks = [
+            [abs_hidden, spread_history],
+            [use_history, sum_hidden],
+            [use_mean, spread_strength],
+            [sigmoid],
+            [use_strength],
+        ]
+        for task in (make_gain, keep_difference, keep_product, keep_sum):
+            for first in range(0, T, 2):
+                tasks.append([lambda task=task, first=first: task(first)])
+        FIRST_TASK = n_steps - T - len(tasks)
 
         acc = [
             acc_pool.tile([P, BANK], F32, name="acc%d" % t, tag="acc%d" % t) for t in range(T)
@@ -207,41 +237,40 @@ def tile_persistentgrucell_pb_k_kernel(
             regrouped = bank[:].rearrange("p (g u r) -> p g r u", g=2, u=2)
             nc.scalar.copy(out=words_out, in_=regrouped)
 
-        def split_halves(unit, first, last):
-            first = max(first, FIRST_SPLIT)
+        def split_words(unit, first):
             tag = "split_" + unit[0]
-            split = stage.tile([P, (last - first) * K_PASS], BF16, name=tag, tag=tag)
-            source = raws[unit][:, first * K_PASS : last * K_PASS]
+            split = stage.tile([P, SLAB - first * K_PASS], BF16, name=tag, tag=tag)
+            source = raws[unit][:, first * K_PASS : SLAB]
             words = split[:].bitcast(F32)
+            splits[unit] = (words, first)
             nc.vector.tensor_copy(
                 out=words.rearrange("p (u w) -> p u w", u=2),
                 in_=source.bitcast(F32).rearrange("p (w u) -> p u w", u=2),
             )
-            return words, first, last
 
-        def bank_blocks(unit, b, split):
-            split_words, first, last = split
+        def bank_blocks(unit, b):
             raw_words = raws[unit][:].bitcast(F32)
+            words, first = splits.get(unit, (None, SLAB_PASSES))
             blocks = []
             for g in (2 * b, 2 * b + 1):
                 for u in range(2):
-                    if g < FIRST_SPLIT:
+                    if g < first:
                         blocks.append(raw_words[:, 2 * P * g + u : 2 * P * (g + 1) : 2])
                     else:
-                        start = (u * (last - first) + g - first) * P
-                        blocks.append(split_words[:, start : start + P])
+                        start = (u * (SLAB_PASSES - first) + g - first) * P
+                        blocks.append(words[:, start : start + P])
             return blocks
 
-        def transpose_x(unit, split):
+        def transpose_x(unit):
             grouped = stage.tile([P, SLAB], BF16, name="x_grouped", align_bytes=64, tag="x_grouped")
             words = grouped[:].bitcast(F32).rearrange("p (g r u) -> p g r u", r=P, u=2)
             for b in range(SLAB_BANKS):
-                transpose_bank(bank_blocks(unit, b, split), words[:, 2 * b : 2 * b + 2])
+                transpose_bank(bank_blocks(unit, b), words[:, 2 * b : 2 * b + 2])
             return grouped
 
         w_grouped = {}
 
-        def transpose_w(c, j, b, blocks):
+        def transpose_w(c, j, b):
             if (c, b) not in w_grouped:
                 grouped = w_pool.tile(
                     [P, 2 * WT * P * 4], BF16, name="w_grouped", align_bytes=64, tag="w_grouped"
@@ -249,7 +278,7 @@ def tile_persistentgrucell_pb_k_kernel(
                 w_grouped[(c, b)] = grouped
             words = w_grouped[(c, b)][:].bitcast(F32)
             words = words.rearrange("p (g j r u) -> p j g r u", j=WT, r=P, u=2)
-            transpose_bank(blocks, words[:, j])
+            transpose_bank(bank_blocks(("w", c, j), b), words[:, j])
 
         w_codes = {}
         w_scales = {}
@@ -296,44 +325,46 @@ def tile_persistentgrucell_pb_k_kernel(
         new_w_tiles(0)
         for b in range(SLAB_BANKS):
             for j in range(WT):
-                unit = ("w", 0, j)
-                transpose_w(0, j, b, bank_blocks(unit, b, split_halves(unit, 2 * b, 2 * b + 2)))
+                transpose_w(0, j, b)
+        for b in range(SLAB_BANKS):
+            quantise_w(0, b)
 
-        w_waiting = [(0, b) for b in range(SLAB_BANKS)]
+        w_waiting = []
         x_waiting = None
         x_ready = {}
-        x_split = {}
-        w_split = {}
+        blends = []
+        ready = []
 
         def w_bank_of(s):
             c, m = steps[s]
             return (c + 1, m % WT, m // WT)
 
         for s in range(n_steps + LAG):
-            if s == 0:
-                x_split[0] = split_halves(("x", 0, 0), 0, SLAB_PASSES)
-                w_split[0] = split_halves(("w", 1, 0), 0, 2)
             if s + 1 < n_steps:
                 c, t = steps[s + 1]
-                x_split[s + 1] = split_halves(("x", c, t), 0, SLAB_PASSES)
+                split_words(("x", c, t), X_FIRST_SPLIT)
                 cw, j, b = w_bank_of(s + 1)
-                if cw < n_slabs:
-                    w_split[s + 1] = split_halves(("w", cw, j), 2 * b, 2 * b + 2)
+                if cw < n_slabs and b == 1:
+                    split_words(("w", cw, j), W_FIRST_SPLIT)
             if x_waiting is not None:
                 x_ready[s - 1] = quantise_x(x_waiting)
                 x_waiting = None
-            for item in w_waiting:
-                quantise_w(*item)
-            w_waiting = []
+            if s < n_steps and steps[s][1] in (0, T - 1):
+                for item in w_waiting:
+                    quantise_w(*item)
+                w_waiting = []
+            for t in blends:
+                blend_and_store(t)
+            blends = []
 
             if s < n_steps:
-                x_waiting = transpose_x(("x",) + steps[s], x_split[s])
+                x_waiting = transpose_x(("x",) + steps[s])
                 c, t = steps[s]
                 cw, j, b = w_bank_of(s)
                 if cw < n_slabs:
                     if (j, b) == (0, 0):
                         new_w_tiles(cw)
-                    transpose_w(cw, j, b, bank_blocks(("w", cw, j), b, w_split[s]))
+                    transpose_w(cw, j, b)
                     if j == WT - 1:
                         w_waiting.append((cw, b))
                 if t == T - 1:
@@ -343,9 +374,16 @@ def tile_persistentgrucell_pb_k_kernel(
                         n_loaded += 1
 
             if s >= LAG:
-                c_old, t_old = steps[s - LAG]
-                multiply(c_old, t_old, *x_ready[s - LAG])
+                ready.append(s - LAG)
+            if s % 2 == 1 or s >= n_steps:
+                for r in ready:
+                    c_old, t_old = steps[r]
+                    multiply(c_old, t_old, *x_ready[r])
+                    if c_old == n_slabs - 1:
+                        blends.append(t_old)
+                ready = []
             if 0 <= s - FIRST_TASK < len(tasks):
-                tasks[s - FIRST_TASK]()
-            if s >= LAG and c_old == n_slabs - 1:
-                blend_and_store(t_old)
+                for task in tasks[s - FIRST_TASK]:
+                    task()
+        for t in blends:
+            blend_and_store(t)

@@ -22,9 +22,10 @@ SLAB_PASSES = SLAB // K_PASS
 SLAB_BANKS = SLAB // K_BANK
 X_FIRST_SPLIT = 1
 W_FIRST_SPLIT = 2
+FIRST_SPLIT_STEP = 3
 LAG = 2
 RAW_BUFS = 28
-FIRST_LOADS = 14
+FIRST_LOADS = 18
 
 
 def tile_persistentgrucell_pb_k_kernel(
@@ -77,9 +78,9 @@ def tile_persistentgrucell_pb_k_kernel(
 
         def load(unit):
             kind, c, r = unit
+            k0 = c * SLAB
             raw = raw_pool.tile([P, SLAB], BF16, tag="raw")
             raws[unit] = raw
-            k0 = c * SLAB
             if kind == "w":
                 nc.sync.dma_start(out=raw[:], in_=Wn[r * P : (r + 1) * P, k0 : k0 + SLAB])
             else:
@@ -188,30 +189,27 @@ def tile_persistentgrucell_pb_k_kernel(
             nc.vector.tensor_tensor(out=cs[:], in0=sig[:], in1=bank[:, H : 2 * H], op=ALU.mult)
             nc.vector.tensor_tensor(out=cs_bn[:], in0=cs[:], in1=bank[:, 0:H], op=ALU.mult)
 
-        def rows_of(tile, first):
-            return tile[:, first * H : (first + 2) * H].rearrange("p (t h) -> p t h", t=2)
+        def rows_of(tile, t):
+            return tile[:, t * H : (t + 1) * H]
 
-        def both(tile):
-            return tile[:].unsqueeze(1).to_broadcast([P, 2, H])
-
-        def make_gain(first):
+        def make_gain(t):
             nc.vector.tensor_tensor(
-                out=rows_of(gain, first), in0=rows_of(upd, first), in1=both(cs), op=ALU.mult
+                out=rows_of(gain, t), in0=rows_of(upd, t), in1=cs[:], op=ALU.mult
             )
 
-        def keep_difference(first):
+        def keep_difference(t):
             nc.vector.tensor_tensor(
-                out=rows_of(keep, first), in0=both(cs_bn), in1=rows_of(hid, first), op=ALU.subtract
+                out=rows_of(keep, t), in0=cs_bn[:], in1=rows_of(hid, t), op=ALU.subtract
             )
 
-        def keep_product(first):
+        def keep_product(t):
             nc.vector.tensor_tensor(
-                out=rows_of(keep, first), in0=rows_of(upd, first), in1=rows_of(keep, first), op=ALU.mult
+                out=rows_of(keep, t), in0=rows_of(upd, t), in1=rows_of(keep, t), op=ALU.mult
             )
 
-        def keep_sum(first):
+        def keep_sum(t):
             nc.vector.tensor_tensor(
-                out=rows_of(keep, first), in0=rows_of(hid, first), in1=rows_of(keep, first), op=ALU.add
+                out=rows_of(keep, t), in0=rows_of(hid, t), in1=rows_of(keep, t), op=ALU.add
             )
 
         tasks = [
@@ -221,10 +219,10 @@ def tile_persistentgrucell_pb_k_kernel(
             [sigmoid],
             [use_strength],
         ]
-        for task in (make_gain, keep_difference, keep_product, keep_sum):
-            for first in range(0, T, 2):
-                tasks.append([lambda task=task, first=first: task(first)])
-        FIRST_TASK = n_steps - T - len(tasks)
+        for t in range(T):
+            for task in (make_gain, keep_difference, keep_product, keep_sum):
+                tasks.append([lambda task=task, t=t: task(t)])
+        FIRST_TASK = n_steps - 1 - len(tasks)
 
         acc = [
             acc_pool.tile([P, BANK], F32, name="acc%d" % t, tag="acc%d" % t) for t in range(T)
@@ -297,10 +295,17 @@ def tile_persistentgrucell_pb_k_kernel(
                 in_=w_grouped[(c, b)][:],
             )
 
-        def quantise_x(grouped):
+        def quantise_x(grouped, parts=1):
             codes = stage.tile([P, SLAB // 4], U32, align_bytes=64)
             scales = stage.tile([P, SLAB // 4], U8, align_bytes=64)
-            nc.vector.quantize_mx(out=codes[:].bitcast(FP8X4), scales=scales[:], in_=grouped[:])
+            n = SLAB // 4 // parts
+            for i in range(parts):
+                cols = slice(i * n, (i + 1) * n)
+                nc.vector.quantize_mx(
+                    out=codes[:, cols].bitcast(FP8X4),
+                    scales=scales[:, cols],
+                    in_=grouped[:, i * n * 4 : (i + 1) * n * 4],
+                )
             return codes, scales
 
         def multiply(c, t, codes, scales):
@@ -319,13 +324,18 @@ def tile_persistentgrucell_pb_k_kernel(
             cols = slice(t * H, (t + 1) * H)
             result = out_pool.tile([P, H], F32, tag="result")
             nc.vector.tensor_tensor(out=result[:], in0=acc[t][:, 0:H], in1=gain[:, cols], op=ALU.mult)
-            nc.vector.tensor_tensor(out=result[:], in0=result[:], in1=keep[:, cols], op=ALU.add)
+            adder = nc.vector if t == T - 1 else nc.gpsimd
+            adder.tensor_tensor(out=result[:], in0=result[:], in1=keep[:, cols], op=ALU.add)
             nc.sync.dma_start(out=out_rows[t], in_=result[:])
 
+        def w_banks(c):
+            if c >= n_slabs:
+                return []
+            return [(c, j, b) for b in range(SLAB_BANKS) for j in range(WT)]
+
         new_w_tiles(0)
-        for b in range(SLAB_BANKS):
-            for j in range(WT):
-                transpose_w(0, j, b)
+        for item in w_banks(0):
+            transpose_w(*item)
         for b in range(SLAB_BANKS):
             quantise_w(0, b)
 
@@ -333,21 +343,22 @@ def tile_persistentgrucell_pb_k_kernel(
         x_waiting = None
         x_ready = {}
         blends = []
-        ready = []
 
-        def w_bank_of(s):
-            c, m = steps[s]
-            return (c + 1, m % WT, m // WT)
+        def w_work(s):
+            c, t = steps[s]
+            banks = w_banks(c + 1)
+            return banks[t : t + 1]
 
         for s in range(n_steps + LAG):
             if s + 1 < n_steps:
                 c, t = steps[s + 1]
-                split_words(("x", c, t), X_FIRST_SPLIT)
-                cw, j, b = w_bank_of(s + 1)
-                if cw < n_slabs and b == 1:
-                    split_words(("w", cw, j), W_FIRST_SPLIT)
+                if s + 1 >= FIRST_SPLIT_STEP:
+                    split_words(("x", c, t), X_FIRST_SPLIT)
+                for cw, j, b in w_work(s + 1):
+                    if 2 * b == W_FIRST_SPLIT:
+                        split_words(("w", cw, j), W_FIRST_SPLIT)
             if x_waiting is not None:
-                x_ready[s - 1] = quantise_x(x_waiting)
+                x_ready[s - 1] = quantise_x(x_waiting, 2 if s >= n_steps else 1)
                 x_waiting = None
             if s < n_steps and steps[s][1] in (0, T - 1):
                 for item in w_waiting:
@@ -360,10 +371,9 @@ def tile_persistentgrucell_pb_k_kernel(
             if s < n_steps:
                 x_waiting = transpose_x(("x",) + steps[s])
                 c, t = steps[s]
-                cw, j, b = w_bank_of(s)
-                if cw < n_slabs:
-                    if (j, b) == (0, 0):
-                        new_w_tiles(cw)
+                if t == 0 and c + 1 < n_slabs:
+                    new_w_tiles(c + 1)
+                for cw, j, b in w_work(s):
                     transpose_w(cw, j, b)
                     if j == WT - 1:
                         w_waiting.append((cw, b))
@@ -374,14 +384,10 @@ def tile_persistentgrucell_pb_k_kernel(
                         n_loaded += 1
 
             if s >= LAG:
-                ready.append(s - LAG)
-            if s % 2 == 1 or s >= n_steps:
-                for r in ready:
-                    c_old, t_old = steps[r]
-                    multiply(c_old, t_old, *x_ready[r])
-                    if c_old == n_slabs - 1:
-                        blends.append(t_old)
-                ready = []
+                c_old, t_old = steps[s - LAG]
+                multiply(c_old, t_old, *x_ready[s - LAG])
+                if c_old == n_slabs - 1:
+                    blends.append(t_old)
             if 0 <= s - FIRST_TASK < len(tasks):
                 for task in tasks[s - FIRST_TASK]:
                     task()

@@ -20,9 +20,9 @@ K_BANK = 1024
 SLAB = 2048
 SLAB_PASSES = SLAB // K_PASS
 SLAB_BANKS = SLAB // K_BANK
-X_FIRST_SPLIT = 1
-W_FIRST_SPLIT = 2
 FIRST_SPLIT_STEP = 3
+IDLE_PASSES = 6
+LAG_PASSES = 2
 LAG = 2
 RAW_BUFS = 28
 FIRST_LOADS = 18
@@ -89,6 +89,24 @@ def tile_persistentgrucell_pb_k_kernel(
                 if width < SLAB:
                     nc.sync.dma_start(out=raw[:, width:SLAB], in_=rh_rows[r])
 
+        ones = const.tile([P, P], BF16)
+        nc.vector.memset(ones[:], 1.0)
+        vectors = const.tile([P, 2 * BANK], BF16)
+        nc.gpsimd.memset(vectors[:], 0.0)
+        ident = const.tile([P, P], F32)
+        make_identity(nc, ident[:])
+        zero = const.tile([P, 1], F32)
+        nc.vector.memset(zero[:], 0.0)
+        nc.scalar.dma_start(out=vectors[0:1, 0:H], in_=bn.unsqueeze(0))
+        nc.scalar.dma_start(out=vectors[0:1, H : 2 * H], in_=connection_strength.unsqueeze(0))
+        nc.scalar.dma_start(out=vectors[0:1, BANK : BANK + H], in_=connection_history.unsqueeze(0))
+        nc.scalar.dma_start(
+            out=vectors[0:1, BANK + H : BANK + H + 1], in_=connection_decay.unsqueeze(0)
+        )
+
+        warm = const.tile([P, 1], F32)
+        nc.scalar.activation(out=warm[:], in_=zero[:], func=ACT.Sigmoid)
+
         for j in range(WT):
             raws[("w", 0, j)] = raw_pool.tile([P, SLAB], BF16, name="raw", tag="raw")
         for b in range(SLAB_BANKS):
@@ -102,29 +120,12 @@ def tile_persistentgrucell_pb_k_kernel(
             load(stream[n_loaded])
             n_loaded += 1
 
-        ident = const.tile([P, P], F32)
-        make_identity(nc, ident[:])
-        ones = const.tile([P, P], BF16)
-        nc.vector.memset(ones[:], 1.0)
-        vectors = const.tile([P, 2 * BANK], BF16)
-        nc.gpsimd.memset(vectors[:], 0.0)
-        zero = const.tile([P, 1], F32)
-        nc.vector.memset(zero[:], 0.0)
-        warm = const.tile([P, 1], F32)
-        nc.scalar.activation(out=warm[:], in_=zero[:], func=ACT.Sigmoid)
-
         hid = const.tile([P, T * H], BF16)
         upd = const.tile([P, T * H], BF16)
 
         def load_small():
             nc.sync.dma_start(out=hid[:], in_=hidden.rearrange("(p t) h -> p (t h)", t=T))
             nc.sync.dma_start(out=upd[:], in_=update.rearrange("(p t) h -> p (t h)", t=T))
-            nc.sync.dma_start(out=vectors[0:1, 0:H], in_=bn.unsqueeze(0))
-            nc.sync.dma_start(out=vectors[0:1, H : 2 * H], in_=connection_strength.unsqueeze(0))
-            nc.sync.dma_start(out=vectors[0:1, BANK : BANK + H], in_=connection_history.unsqueeze(0))
-            nc.sync.dma_start(
-                out=vectors[0:1, BANK + H : BANK + H + 1], in_=connection_decay.unsqueeze(0)
-            )
 
         load_small()
         while n_loaded < RAW_BUFS:
@@ -133,6 +134,7 @@ def tile_persistentgrucell_pb_k_kernel(
 
         habs = const.tile([P, T * H], BF16)
         cs = const.tile([P, H], F32)
+        bn_strength = const.tile([P, BANK], F32)
         cs_bn = const.tile([P, H], F32)
         ch = const.tile([P, H], F32)
         decay = const.tile([P, 1], F32)
@@ -150,15 +152,14 @@ def tile_persistentgrucell_pb_k_kernel(
         def abs_hidden():
             nc.scalar.activation(out=habs[:], in_=hid[:], func=ACT.Abs)
 
-        def spread_history():
-            banks["history"] = spread(slice(BANK, 2 * BANK))
-
-        def use_history():
-            bank = banks["history"]
+        def spread_vectors():
+            bank = spread(slice(BANK, 2 * BANK))
             nc.vector.tensor_copy(out=decay[:], in_=bank[:, H : H + 1])
             nc.vector.tensor_scalar(
                 out=ch[:], in0=bank[:, 0:H], scalar1=decay[:, 0:1], scalar2=None, op0=ALU.mult
             )
+            bank = spread(slice(0, BANK))
+            nc.vector.tensor_copy(out=bn_strength[:], in_=bank[:])
 
         def sum_hidden():
             bank = bank_pool.tile([P, BANK], F32, tag="bank")
@@ -181,13 +182,13 @@ def tile_persistentgrucell_pb_k_kernel(
         def sigmoid():
             nc.scalar.activation(out=sig[:], in_=ch[:], func=ACT.Sigmoid)
 
-        def spread_strength():
-            banks["strength"] = spread(slice(0, BANK))
+        def make_cs():
+            nc.vector.tensor_tensor(
+                out=cs[:], in0=sig[:], in1=bn_strength[:, H : 2 * H], op=ALU.mult
+            )
 
-        def use_strength():
-            bank = banks["strength"]
-            nc.vector.tensor_tensor(out=cs[:], in0=sig[:], in1=bank[:, H : 2 * H], op=ALU.mult)
-            nc.vector.tensor_tensor(out=cs_bn[:], in0=cs[:], in1=bank[:, 0:H], op=ALU.mult)
+        def make_cs_bn():
+            nc.vector.tensor_tensor(out=cs_bn[:], in0=cs[:], in1=bn_strength[:, 0:H], op=ALU.mult)
 
         def rows_of(tile, t):
             return tile[:, t * H : (t + 1) * H]
@@ -213,16 +214,17 @@ def tile_persistentgrucell_pb_k_kernel(
             )
 
         tasks = [
-            [abs_hidden, spread_history],
-            [use_history, sum_hidden],
-            [use_mean, spread_strength],
+            [abs_hidden],
+            [sum_hidden],
+            [use_mean],
             [sigmoid],
-            [use_strength],
+            [make_cs],
+            [make_cs_bn],
         ]
         for t in range(T):
             for task in (make_gain, keep_difference, keep_product, keep_sum):
                 tasks.append([lambda task=task, t=t: task(t)])
-        FIRST_TASK = n_steps - 1 - len(tasks)
+        FIRST_TASK = n_steps - 2 - len(tasks)
 
         acc = [
             acc_pool.tile([P, BANK], F32, name="acc%d" % t, tag="acc%d" % t) for t in range(T)
@@ -235,29 +237,21 @@ def tile_persistentgrucell_pb_k_kernel(
             regrouped = bank[:].rearrange("p (g u r) -> p g r u", g=2, u=2)
             nc.scalar.copy(out=words_out, in_=regrouped)
 
-        def split_words(unit, first):
-            tag = "split_" + unit[0]
-            split = stage.tile([P, SLAB - first * K_PASS], BF16, name=tag, tag=tag)
-            source = raws[unit][:, first * K_PASS : SLAB]
-            words = split[:].bitcast(F32)
-            splits[unit] = (words, first)
+        def split_words(unit):
+            split = stage.tile([P, 2, SLAB // 4], F32, tag="split")
+            splits[unit] = split
             nc.vector.tensor_copy(
-                out=words.rearrange("p (u w) -> p u w", u=2),
-                in_=source.bitcast(F32).rearrange("p (w u) -> p u w", u=2),
+                out=split[:], in_=raws[unit][:].bitcast(F32).rearrange("p (w u) -> p u w", u=2)
             )
 
         def bank_blocks(unit, b):
-            raw_words = raws[unit][:].bitcast(F32)
-            words, first = splits.get(unit, (None, SLAB_PASSES))
-            blocks = []
-            for g in (2 * b, 2 * b + 1):
-                for u in range(2):
-                    if g < first:
-                        blocks.append(raw_words[:, 2 * P * g + u : 2 * P * (g + 1) : 2])
-                    else:
-                        start = (u * (SLAB_PASSES - first) + g - first) * P
-                        blocks.append(words[:, start : start + P])
-            return blocks
+            if unit in splits:
+                words = splits[unit]
+            else:
+                words = raws[unit][:].bitcast(F32).rearrange("p (w u) -> p u w", u=2)
+            return [
+                words[:, u, g * P : (g + 1) * P] for g in (2 * b, 2 * b + 1) for u in range(2)
+            ]
 
         def transpose_x(unit):
             grouped = stage.tile([P, SLAB], BF16, name="x_grouped", align_bytes=64, tag="x_grouped")
@@ -334,8 +328,19 @@ def tile_persistentgrucell_pb_k_kernel(
             return [(c, j, b) for b in range(SLAB_BANKS) for j in range(WT)]
 
         new_w_tiles(0)
-        for item in w_banks(0):
+        dummy = const.tile([P, BANK], BF16)
+        nc.vector.memset(dummy[:], 0.0)
+
+        def warm_up(n):
+            for i in range(n):
+                bank = bank_pool.tile([P, BANK], F32, tag="bank")
+                nc.tensor.matmul(bank[:], lhsT=ones[:], rhs=dummy[:], start=True, stop=True)
+
+        warm_up(IDLE_PASSES)
+        for n, item in enumerate(w_banks(0)):
             transpose_w(*item)
+            if n == 1:
+                spread_vectors()
         for b in range(SLAB_BANKS):
             quantise_w(0, b)
 
@@ -353,10 +358,7 @@ def tile_persistentgrucell_pb_k_kernel(
             if s + 1 < n_steps:
                 c, t = steps[s + 1]
                 if s + 1 >= FIRST_SPLIT_STEP:
-                    split_words(("x", c, t), X_FIRST_SPLIT)
-                for cw, j, b in w_work(s + 1):
-                    if 2 * b == W_FIRST_SPLIT:
-                        split_words(("w", cw, j), W_FIRST_SPLIT)
+                    split_words(("x", c, t))
             if x_waiting is not None:
                 x_ready[s - 1] = quantise_x(x_waiting, 2 if s >= n_steps else 1)
                 x_waiting = None
@@ -383,6 +385,8 @@ def tile_persistentgrucell_pb_k_kernel(
                         load(stream[n_loaded])
                         n_loaded += 1
 
+            if s < LAG:
+                warm_up(LAG_PASSES)
             if s >= LAG:
                 c_old, t_old = steps[s - LAG]
                 multiply(c_old, t_old, *x_ready[s - LAG])

from contextlib import ExitStack

import concourse.mybir as mybir
from concourse.masks import make_identity

FLOPS = 2 * 512 * 256 * 16384

F32 = mybir.dt.float32
BF16 = mybir.dt.bfloat16
U32 = mybir.dt.uint32
U8 = mybir.dt.uint8
FP8X4 = mybir.dt.float8_e4m3fn_x4
ALU = mybir.AluOpType
ACT = mybir.ActivationFunctionType

P = 128
K_PASS = 512
BANK = 512
K_BANK = 1024
SLAB = 2048
SLAB_PASSES = SLAB // K_PASS
SLAB_BANKS = SLAB // K_BANK
FIRST_SPLIT_STEP = 3
IDLE_PASSES = 6
LAG_PASSES = 2
LAG = 2
RAW_BUFS = 28
FIRST_LOADS = 18


def tile_persistentgrucell_pb_k_kernel(
    tc,
    x,
    rh,
    update,
    hidden,
    Wn,
    bn,
    connection_strength,
    connection_decay,
    connection_history,
    out,
):
    nc = tc.nc
    B, I = x.shape
    H = rh.shape[1]
    K = I + H
    T = B // P
    WT = H // P
    n_slabs = K // SLAB

    x_rows = x.rearrange("(p t) k -> t p k", t=T)
    rh_rows = rh.rearrange("(p t) k -> t p k", t=T)
    out_rows = out.rearrange("(p t) h -> t p h", t=T)

    stream = [("w", 0, j) for j in range(WT)]
    for c in range(n_slabs):
        for t in range(T):
            stream.append(("x", c, t))
            if c + 1 < n_slabs and t < WT:
                stream.append(("w", c + 1, t))

    steps = [(c, t) for c in range(n_slabs) for t in range(T)]
    n_steps = len(steps)

    with ExitStack() as ctx:
        ctx.enter_context(tc.manual_schedule())
        const = ctx.enter_context(tc.tile_pool(name="const", bufs=1))
        raw_pool = ctx.enter_context(tc.tile_pool(name="raw", bufs=RAW_BUFS))
        stage = ctx.enter_context(tc.tile_pool(name="stage", bufs=LAG + 2))
        w_pool = ctx.enter_context(tc.tile_pool(name="wq", bufs=3))
        out_pool = ctx.enter_context(tc.tile_pool(name="outs", bufs=T))
        acc_pool = ctx.enter_context(tc.psum_pool(name="acc", bufs=1))
        bank_pool = ctx.enter_context(tc.psum_pool(name="banks", bufs=4))

        raws = {}
        splits = {}

        def load(unit):
            kind, c, r = unit
            k0 = c * SLAB
            raw = raw_pool.tile([P, SLAB], BF16, tag="raw")
            raws[unit] = raw
            if kind == "w":
                nc.sync.dma_start(out=raw[:], in_=Wn[r * P : (r + 1) * P, k0 : k0 + SLAB])
            else:
                width = min(SLAB, I - k0)
                nc.sync.dma_start(out=raw[:, 0:width], in_=x_rows[r][:, k0 : k0 + width])
                if width < SLAB:
                    nc.sync.dma_start(out=raw[:, width:SLAB], in_=rh_rows[r])

        ones = const.tile([P, P], BF16)
        nc.vector.memset(ones[:], 1.0)
        vectors = const.tile([P, 2 * BANK], BF16)
        nc.gpsimd.memset(vectors[:], 0.0)
        ident = const.tile([P, P], F32)
        make_identity(nc, ident[:])
        zero = const.tile([P, 1], F32)
        nc.vector.memset(zero[:], 0.0)
        nc.scalar.dma_start(out=vectors[0:1, 0:H], in_=bn.unsqueeze(0))
        nc.scalar.dma_start(out=vectors[0:1, H : 2 * H], in_=connection_strength.unsqueeze(0))
        nc.scalar.dma_start(out=vectors[0:1, BANK : BANK + H], in_=connection_history.unsqueeze(0))
        nc.scalar.dma_start(
            out=vectors[0:1, BANK + H : BANK + H + 1], in_=connection_decay.unsqueeze(0)
        )

        warm = const.tile([P, 1], F32)
        nc.scalar.activation(out=warm[:], in_=zero[:], func=ACT.Sigmoid)

        for j in range(WT):
            raws[("w", 0, j)] = raw_pool.tile([P, SLAB], BF16, name="raw", tag="raw")
        for b in range(SLAB_BANKS):
            for j in range(WT):
                cols = slice(b * K_BANK, (b + 1) * K_BANK)
                nc.sync.dma_start(
                    out=raws[("w", 0, j)][:, cols], in_=Wn[j * P : (j + 1) * P, cols]
                )
        n_loaded = WT
        while n_loaded < FIRST_LOADS:
            load(stream[n_loaded])
            n_loaded += 1

        hid = const.tile([P, T * H], BF16)
        upd = const.tile([P, T * H], BF16)

        def load_small():
            nc.sync.dma_start(out=hid[:], in_=hidden.rearrange("(p t) h -> p (t h)", t=T))
            nc.sync.dma_start(out=upd[:], in_=update.rearrange("(p t) h -> p (t h)", t=T))

        load_small()
        while n_loaded < RAW_BUFS:
            load(stream[n_loaded])
            n_loaded += 1

        habs = const.tile([P, T * H], BF16)
        cs = const.tile([P, H], F32)
        bn_strength = const.tile([P, BANK], F32)
        cs_bn = const.tile([P, H], F32)
        ch = const.tile([P, H], F32)
        decay = const.tile([P, 1], F32)
        sig = const.tile([P, H], F32)
        gain = const.tile([P, T * H], F32)
        keep = const.tile([P, T * H], F32)

        def spread(cols):
            bank = bank_pool.tile([P, BANK], F32, tag="bank")
            nc.tensor.matmul(bank[:], lhsT=ones[:], rhs=vectors[:, cols], start=True, stop=True)
            return bank

        banks = {}

        def abs_hidden():
            nc.scalar.activation(out=habs[:], in_=hid[:], func=ACT.Abs)

        def spread_vectors():
            bank = spread(slice(BANK, 2 * BANK))
            nc.vector.tensor_copy(out=decay[:], in_=bank[:, H : H + 1])
            nc.vector.tensor_scalar(
                out=ch[:], in0=bank[:, 0:H], scalar1=decay[:, 0:1], scalar2=None, op0=ALU.mult
            )
            bank = spread(slice(0, BANK))
            nc.vector.tensor_copy(out=bn_strength[:], in_=bank[:])

        def sum_hidden():
            bank = bank_pool.tile([P, BANK], F32, tag="bank")
            banks["mean"] = bank
            for t in range(T):
                nc.tensor.matmul(
                    bank[:, 0:H],
                    lhsT=ones[:],
                    rhs=habs[:, t * H : (t + 1) * H],
                    start=(t == 0),
                    stop=(t == T - 1),
                )

        def use_mean():
            bank = banks["mean"]
            nc.vector.scalar_tensor_tensor(
                out=ch[:], in0=bank[:, 0:H], scalar=1.0 / B, in1=ch[:], op0=ALU.mult, op1=ALU.add
            )

        def sigmoid():
            nc.scalar.activation(out=sig[:], in_=ch[:], func=ACT.Sigmoid)

        def make_cs():
            nc.vector.tensor_tensor(
                out=cs[:], in0=sig[:], in1=bn_strength[:, H : 2 * H], op=ALU.mult
            )

        def make_cs_bn():
            nc.vector.tensor_tensor(out=cs_bn[:], in0=cs[:], in1=bn_strength[:, 0:H], op=ALU.mult)

        def rows_of(tile, t):
            return tile[:, t * H : (t + 1) * H]

        def make_gain(t):
            nc.vector.tensor_tensor(
                out=rows_of(gain, t), in0=rows_of(upd, t), in1=cs[:], op=ALU.mult
            )

        def keep_difference(t):
            nc.vector.tensor_tensor(
                out=rows_of(keep, t), in0=cs_bn[:], in1=rows_of(hid, t), op=ALU.subtract
            )

        def keep_product(t):
            nc.vector.tensor_tensor(
                out=rows_of(keep, t), in0=rows_of(upd, t), in1=rows_of(keep, t), op=ALU.mult
            )

        def keep_sum(t):
            nc.vector.tensor_tensor(
                out=rows_of(keep, t), in0=rows_of(hid, t), in1=rows_of(keep, t), op=ALU.add
            )

        tasks = [
            [abs_hidden],
            [sum_hidden],
            [use_mean],
            [sigmoid],
            [make_cs],
            [make_cs_bn],
        ]
        for t in range(T):
            for task in (make_gain, keep_difference, keep_product, keep_sum):
                tasks.append([lambda task=task, t=t: task(t)])
        FIRST_TASK = n_steps - 2 - len(tasks)

        acc = [
            acc_pool.tile([P, BANK], F32, name="acc%d" % t, tag="acc%d" % t) for t in range(T)
        ]

        def transpose_bank(blocks, words_out):
            bank = bank_pool.tile([P, BANK], F32, tag="bank")
            for q in range(4):
                nc.tensor.transpose(bank[:, q * P : (q + 1) * P], blocks[q], ident[:])
            regrouped = bank[:].rearrange("p (g u r) -> p g r u", g=2, u=2)
            nc.scalar.copy(out=words_out, in_=regrouped)

        def split_words(unit):
            split = stage.tile([P, 2, SLAB // 4], F32, tag="split")
            splits[unit] = split
            nc.vector.tensor_copy(
                out=split[:], in_=raws[unit][:].bitcast(F32).rearrange("p (w u) -> p u w", u=2)
            )

        def bank_blocks(unit, b):
            if unit in splits:
                words = splits[unit]
            else:
                words = raws[unit][:].bitcast(F32).rearrange("p (w u) -> p u w", u=2)
            return [
                words[:, u, g * P : (g + 1) * P] for g in (2 * b, 2 * b + 1) for u in range(2)
            ]

        def transpose_x(unit):
            grouped = stage.tile([P, SLAB], BF16, name="x_grouped", align_bytes=64, tag="x_grouped")
            words = grouped[:].bitcast(F32).rearrange("p (g r u) -> p g r u", r=P, u=2)
            for b in range(SLAB_BANKS):
                transpose_bank(bank_blocks(unit, b), words[:, 2 * b : 2 * b + 2])
            return grouped

        w_grouped = {}

        def transpose_w(c, j, b):
            if (c, b) not in w_grouped:
                grouped = w_pool.tile(
                    [P, 2 * WT * P * 4], BF16, name="w_grouped", align_bytes=64, tag="w_grouped"
                )
                w_grouped[(c, b)] = grouped
            words = w_grouped[(c, b)][:].bitcast(F32)
            words = words.rearrange("p (g j r u) -> p j g r u", j=WT, r=P, u=2)
            transpose_bank(bank_blocks(("w", c, j), b), words[:, j])

        w_codes = {}
        w_scales = {}

        def new_w_tiles(c):
            codes = w_pool.tile([P, SLAB_PASSES * H], U32, align_bytes=64, tag="w_codes")
            scales = w_pool.tile([P, SLAB_PASSES * H], U8, align_bytes=64, tag="w_scales")
            w_codes[c] = codes
            w_scales[c] = scales

        def quantise_w(c, b):
            cols = slice(b * 2 * H, (b + 1) * 2 * H)
            nc.vector.quantize_mx(
                out=w_codes[c][:, cols].bitcast(FP8X4),
                scales=w_scales[c][:, cols],
                in_=w_grouped[(c, b)][:],
            )

        def quantise_x(grouped, parts=1):
            codes = stage.tile([P, SLAB // 4], U32, align_bytes=64)
            scales = stage.tile([P, SLAB // 4], U8, align_bytes=64)
            n = SLAB // 4 // parts
            for i in range(parts):
                cols = slice(i * n, (i + 1) * n)
                nc.vector.quantize_mx(
                    out=codes[:, cols].bitcast(FP8X4),
                    scales=scales[:, cols],
                    in_=grouped[:, i * n * 4 : (i + 1) * n * 4],
                )
            return codes, scales

        def multiply(c, t, codes, scales):
            for g in range(SLAB_PASSES):
                nc.tensor.matmul_mx(
                    out=acc[t][:, 0:H],
                    lhsT=codes[:, g * P : (g + 1) * P].bitcast(FP8X4),
                    lhsT_scale=scales[:, g * P : (g + 1) * P],
                    rhs=w_codes[c][:, g * H : (g + 1) * H].bitcast(FP8X4),
                    rhs_scale=w_scales[c][:, g * H : (g + 1) * H],
                    start=(c == 0 and g == 0),
                    stop=(c == n_slabs - 1 and g == SLAB_PASSES - 1),
                )

        def blend_and_store(t):
            cols = slice(t * H, (t + 1) * H)
            result = out_pool.tile([P, H], F32, tag="result")
            nc.vector.tensor_tensor(out=result[:], in0=acc[t][:, 0:H], in1=gain[:, cols], op=ALU.mult)
            adder = nc.vector if t == T - 1 else nc.gpsimd
            adder.tensor_tensor(out=result[:], in0=result[:], in1=keep[:, cols], op=ALU.add)
            nc.sync.dma_start(out=out_rows[t], in_=result[:])

        def w_banks(c):
            if c >= n_slabs:
                return []
            return [(c, j, b) for b in range(SLAB_BANKS) for j in range(WT)]

        new_w_tiles(0)
        dummy = const.tile([P, BANK], BF16)
        nc.vector.memset(dummy[:], 0.0)

        def warm_up(n):
            for i in range(n):
                bank = bank_pool.tile([P, BANK], F32, tag="bank")
                nc.tensor.matmul(bank[:], lhsT=ones[:], rhs=dummy[:], start=True, stop=True)

        warm_up(IDLE_PASSES)
        for n, item in enumerate(w_banks(0)):
            transpose_w(*item)
            if n == 1:
                spread_vectors()
        for b in range(SLAB_BANKS):
            quantise_w(0, b)

        w_waiting = []
        x_waiting = None
        x_ready = {}
        blends = []

        def w_work(s):
            c, t = steps[s]
            banks = w_banks(c + 1)
            return banks[t : t + 1]

        for s in range(n_steps + LAG):
            if s + 1 < n_steps:
                c, t = steps[s + 1]
                if s + 1 >= FIRST_SPLIT_STEP:
                    split_words(("x", c, t))
            if x_waiting is not None:
                x_ready[s - 1] = quantise_x(x_waiting, 2 if s >= n_steps else 1)
                x_waiting = None
            if s < n_steps and steps[s][1] in (0, T - 1):
                for item in w_waiting:
                    quantise_w(*item)
                w_waiting = []
            for t in blends:
                blend_and_store(t)
            blends = []

            if s < n_steps:
                x_waiting = transpose_x(("x",) + steps[s])
                c, t = steps[s]
                if t == 0 and c + 1 < n_slabs:
                    new_w_tiles(c + 1)
                for cw, j, b in w_work(s):
                    transpose_w(cw, j, b)
                    if j == WT - 1:
                        w_waiting.append((cw, b))
                if t == T - 1:
                    n_free = min(len(stream), stream.index(("x", c, t)) + 1 + RAW_BUFS)
                    while n_loaded < n_free:
                        load(stream[n_loaded])
                        n_loaded += 1

            if s < LAG:
                warm_up(LAG_PASSES)
            if s >= LAG:
                c_old, t_old = steps[s - LAG]
                multiply(c_old, t_old, *x_ready[s - LAG])
                if c_old == n_slabs - 1:
                    blends.append(t_old)
            if 0 <= s - FIRST_TASK < len(tasks):
                for task in tasks[s - FIRST_TASK]:
                    task()
        for t in blends:
            blend_and_store(t)
